import numpy as np
import ml_dtypes


def mxq(x, axis, fmt="e4m3"):
    dtype, down = {"e4m3": (ml_dtypes.float8_e4m3fn, 7), "e5m2": (ml_dtypes.float8_e5m2, 14)}[fmt]
    v = np.moveaxis(np.asarray(x, np.float32).astype(ml_dtypes.bfloat16).astype(np.float64), axis, -1)
    blocks = v.reshape(v.shape[:-1] + (-1, 32))
    amax = np.abs(blocks).max(-1, keepdims=True)
    byte = np.maximum(np.where(amax > 0, np.frexp(amax)[1] - 1 + 127, 0) - down, 1)
    scale = np.exp2(byte - 127.0)
    codes = (blocks / scale).astype(np.float32).astype(dtype).astype(np.float64)
    return np.moveaxis((codes * scale).reshape(v.shape), -1, axis)


WIDE = False


def mx_kscale(k):
    if not WIDE:
        return np.ones(k)
    levels = np.array([10, -10, 5, -5, 0])
    a = np.random.permutation(np.resize(levels, k // 512 * 4)).reshape(k // 512, 4)
    idx = np.arange(k)
    return np.exp2(a[idx // 512, idx % 128 // 32])


BF16 = ml_dtypes.bfloat16


def bf(x):
    return np.asarray(x, np.float32).astype(BF16)


def f64(x):
    return np.asarray(x).astype(np.float64)


B, N, F, D, DIM = 8, 1024, 1024, 512, 32
EPS = 1e-6
RAD = 3.0


def expmap0_full(us):
    r = np.sqrt((us * us).sum(-1, keepdims=True))
    rs = np.maximum(r, EPS)
    x0 = 0.5 * (np.exp(r) + np.exp(-r))
    xs = (0.5 * (np.exp(rs) - np.exp(-rs)) / rs) * us
    return np.concatenate([x0, xs], axis=-1)


def setup_inputs():
    s = mx_kscale(F)
    amp = 0.5 + 0.5 * np.random.random((B, N, 1))
    return {"x": bf(np.random.standard_normal((B, N, F)) * amp * s),
            "w_sp": bf(np.random.standard_normal((F, D)) * RAD / np.sqrt(D * F) / s[:, None])}


def reference(x, w_sp):
    us = mxq(f64(x), 2, "e4m3") @ mxq(f64(w_sp), 0, "e4m3")
    return expmap0_full(us)

@@ -1,0 +1,197 @@
+import concourse.mybir as mybir
+from concourse.masks import make_identity
+
+BF16 = mybir.dt.bfloat16
+F32 = mybir.dt.float32
+U32 = mybir.dt.uint32
+U8 = mybir.dt.uint8
+FP8X4 = mybir.dt.float8_e4m3fn_x4
+ACT = mybir.ActivationFunctionType
+ALU = mybir.AluOpType
+
+P = 128
+GRAPHS, NODES, FEATURES, DIMS = 8, 1024, 1024, 512
+PACK = 4
+K_PASS = P * PACK
+PASSES = FEATURES // K_PASS
+HALVES = 2
+TILES = NODES // P
+PAIR = 2
+PAIRS = TILES // PAIR
+N_PAIRS = GRAPHS * PAIRS
+TILE_COLS = PASSES * P * PACK
+TILE_WORDS = PASSES * P
+EPS = 1e-6
+
+FLOPS = 2 * GRAPHS * NODES * FEATURES * DIMS
+
+
+def tile_hgcn_pb_t_kernel(tc, x, w_sp, out):
+    nc = tc.nc
+    with (
+        tc.tile_pool(name="const", bufs=1) as const,
+        tc.tile_pool(name="x_pool", bufs=GRAPHS) as x_pool,
+        tc.tile_pool(name="out_pool", bufs=3) as out_pool,
+        tc.tile_pool(name="mx_pool", bufs=3) as mx_pool,
+        tc.tile_pool(name="small", bufs=4) as small,
+        tc.psum_pool(name="xt_pool", bufs=PAIR) as xt_pool,
+        tc.psum_pool(name="us_pool", bufs=3 * PAIR) as us_pool,
+        tc.manual_schedule(),
+    ):
+        x_sb, out_sb = {}, {}
+        x_t, grouped, codes, scales, us = {}, {}, {}, {}, {}
+        sumsq, radius, e_pos, e_neg, factor = {}, {}, {}, {}, {}
+
+        def load_nodes(b, first_tile, n_tiles):
+            rows = x[b].rearrange("(p j) k -> p j k", j=TILES)
+            cut = slice(first_tile, first_tile + n_tiles)
+            nc.sync.dma_start(out=x_sb[b][:, cut, :], in_=rows[:, cut, :])
+
+        for b in range(GRAPHS):
+            x_sb[b] = x_pool.tile([P, TILES, FEATURES], BF16, name="x_sb")
+
+        load_nodes(0, 0, PAIR)
+        w_raw = const.tile([P, PASSES, PACK, DIMS], BF16)
+        nc.sync.dma_start(
+            out=w_raw[:].rearrange("p g (u e) d -> p (g u) (e d)", u=HALVES),
+            in_=w_sp.rearrange("(c p e) d -> p c (e d)", c=PASSES * HALVES, p=P),
+        )
+        for q in range(1, PAIRS):
+            load_nodes(0, PAIR * q, PAIR)
+        for b in range(1, GRAPHS):
+            load_nodes(b, 0, TILES)
+
+        ident = const.tile([P, P], F32)
+        make_identity(nc, ident[:])
+        half = const.tile([P, PAIR], F32)
+        nc.gpsimd.memset(half[:], 0.5)
+
+        w_grouped = const.tile([P, PASSES, DIMS, PACK], BF16, align_bytes=64)
+        for g in range(PASSES):
+            nc.vector.tensor_copy(out=w_grouped[:, g], in_=w_raw[:, g].rearrange("p t d -> p d t"))
+        w_codes = const.tile([P, PASSES * DIMS], U32, align_bytes=64)
+        w_scales = const.tile([P, PASSES * DIMS], U8, align_bytes=64)
+        nc.vector.quantize_mx(
+            out=w_codes[:].bitcast(FP8X4),
+            scales=w_scales[:],
+            in_=w_grouped[:].rearrange("p g d t -> p (g d t)"),
+        )
+
+        def transpose_pair(n):
+            b, q = divmod(n, PAIRS)
+            for i in range(PAIR):
+                words = x_sb[b][:, PAIR * q + i, :].bitcast(F32)
+                bank = xt_pool.tile([P, PASSES, HALVES, P], F32, name="x_t")
+                for g in range(PASSES):
+                    for u in range(HALVES):
+                        first = (g * HALVES + u) * P
+                        nc.tensor.transpose(bank[:, g, u, :], words[:, first : first + P], ident[:])
+                x_t[n, i] = bank
+
+        def copy_out_pair(n):
+            grouped[n] = mx_pool.tile([P, PAIR * TILE_COLS], BF16, align_bytes=64, name="grouped")
+            for i in range(PAIR):
+                dst = grouped[n][:, i * TILE_COLS : (i + 1) * TILE_COLS].bitcast(F32)
+                dst = dst.rearrange("p (g r u) -> p g r u", g=PASSES, u=HALVES)
+                src = x_t[n, i][:].rearrange("p g u r -> p g r u")
+                if i == 1 and n % 2 == 1:
+                    nc.vector.tensor_copy(out=dst, in_=src)
+                else:
+                    nc.scalar.copy(out=dst, in_=src)
+
+        def quantise_pair(n):
+            codes[n] = mx_pool.tile([P, PAIR * TILE_WORDS], U32, align_bytes=64, name="codes")
+            scales[n] = mx_pool.tile([P, PAIR * TILE_WORDS], U8, align_bytes=64, name="scales")
+            nc.vector.quantize_mx(out=codes[n][:].bitcast(FP8X4), scales=scales[n][:], in_=grouped[n][:])
+
+        def multiply_pair(n):
+            for i in range(PAIR):
+                us[n, i] = us_pool.tile([P, DIMS], F32, name="us")
+                for g in range(PASSES):
+                    nodes = slice((i * PASSES + g) * P, (i * PASSES + g + 1) * P)
+                    dims = slice(g * DIMS, (g + 1) * DIMS)
+                    nc.tensor.matmul_mx(
+                        out=us[n, i][:],
+                        lhsT=codes[n][:, nodes].bitcast(FP8X4),
+                        lhsT_scale=scales[n][:, nodes],
+                        rhs=w_codes[:, dims].bitcast(FP8X4),
+                        rhs_scale=w_scales[:, dims],
+                        start=(g == 0),
+                        stop=(g == PASSES - 1),
+                    )
+
+        def sum_squares(n, i):
+            if i == 0:
+                sumsq[n] = small.tile([P, PAIR], F32, name="sumsq")
+            squares = small.tile([P, DIMS], BF16, name="squares")
+            nc.scalar.activation(out=squares[:], in_=us[n, i][:], func=ACT.Square, accum_out=sumsq[n][:, i : i + 1])
+
+        def take_root(n):
+            clamped = small.tile([P, PAIR], F32, name="clamped")
+            nc.gpsimd.tensor_scalar(out=clamped[:], in0=sumsq[n][:], scalar1=EPS * EPS, scalar2=None, op0=ALU.max)
+            radius[n] = small.tile([P, PAIR], F32, name="radius")
+            nc.gpsimd.tensor_tensor(out=radius[n][:], in0=clamped[:], in1=half[:], op=ALU.pow)
+
+        def exponentials(n):
+            e_pos[n] = small.tile([P, PAIR], F32, name="e_pos")
+            e_neg[n] = small.tile([P, PAIR], F32, name="e_neg")
+            nc.scalar.activation(out=e_pos[n][:], in_=radius[n][:], func=ACT.Exp)
+            nc.scalar.activation(out=e_neg[n][:], in_=radius[n][:], func=ACT.Exp, scale=-1.0)
+
+        def factors(n):
+            b, q = divmod(n, PAIRS)
+            if q == 0:
+                out_sb[b] = out_pool.tile([P, TILES, 1 + DIMS], F32, name="out_sb")
+            inverse = small.tile([P, PAIR], F32, name="inverse")
+            nc.vector.reciprocal(out=inverse[:], in_=radius[n][:])
+            diff = small.tile([P, PAIR], F32, name="diff")
+            nc.vector.tensor_sub(out=diff[:], in0=e_pos[n][:], in1=e_neg[n][:])
+            factor[n] = small.tile([P, PAIR], F32, name="factor")
+            nc.vector.tensor_mul(out=factor[n][:], in0=diff[:], in1=inverse[:])
+            nc.vector.scalar_tensor_tensor(
+                out=out_sb[b][:, PAIR * q : PAIR * (q + 1), 0],
+                in0=diff[:],
+                scalar=0.5,
+                in1=e_neg[n][:],
+                op0=ALU.mult,
+                op1=ALU.add,
+            )
+
+        def scale_pair(n):
+            b, q = divmod(n, PAIRS)
+            for i in range(PAIR):
+                nc.vector.tensor_scalar(
+                    out=out_sb[b][:, PAIR * q + i, 1:],
+                    in0=us[n, i][:],
+                    scalar1=factor[n][:, i : i + 1],
+                    scalar2=0.5,
+                    op0=ALU.mult,
+                    op1=ALU.mult,
+                )
+
+        def store_graph(b):
+            nc.scalar.dma_start(out=out[b].rearrange("(p j) d -> p j d", j=TILES), in_=out_sb[b][:])
+
+        def live(n):
+            return 0 <= n < N_PAIRS
+
+        for s in range(N_PAIRS + 4):
+            if live(s - 4):
+                scale_pair(s - 4)
+            if live(s):
+                transpose_pair(s)
+                copy_out_pair(s)
+            if live(s - 1):
+                quantise_pair(s - 1)
+            if live(s - 2):
+                multiply_pair(s - 2)
+                sum_squares(s - 2, 0)
+            if live(s - 3):
+                exponentials(s - 3)
+            if live(s - 2):
+                sum_squares(s - 2, 1)
+                take_root(s - 2)
+            if live(s - 3):
+                factors(s - 3)
+            if live(s - 4) and (s - 4) % PAIRS == PAIRS - 1:
+                store_graph((s - 4) // PAIRS)

@@ -22,6 +22,8 @@ N_PAIRS = GRAPHS * PAIRS
 TILE_COLS = PASSES * P * PACK
 TILE_WORDS = PASSES * P
 EPS = 1e-6
+TWO_SINH_EPS = 2.0 * EPS * (1.0 + EPS * EPS / 6.0)
+PIECE = 1024
 
 FLOPS = 2 * GRAPHS * NODES * FEATURES * DIMS
 
@@ -32,7 +34,7 @@ def tile_hgcn_pb_t_kernel(tc, x, w_sp, out):
         tc.tile_pool(name="const", bufs=1) as const,
         tc.tile_pool(name="x_pool", bufs=GRAPHS) as x_pool,
         tc.tile_pool(name="out_pool", bufs=3) as out_pool,
-        tc.tile_pool(name="mx_pool", bufs=3) as mx_pool,
+        tc.tile_pool(name="mx_pool", bufs=4) as mx_pool,
         tc.tile_pool(name="small", bufs=4) as small,
         tc.psum_pool(name="xt_pool", bufs=PAIR) as xt_pool,
         tc.psum_pool(name="us_pool", bufs=3 * PAIR) as us_pool,
@@ -40,7 +42,7 @@ def tile_hgcn_pb_t_kernel(tc, x, w_sp, out):
     ):
         x_sb, out_sb = {}, {}
         x_t, grouped, codes, scales, us = {}, {}, {}, {}, {}
-        sumsq, radius, e_pos, e_neg, factor = {}, {}, {}, {}, {}
+        sumsq, radius, clamped, e_pos, e_neg, inverse, diff, sinh = {}, {}, {}, {}, {}, {}, {}, {}
 
         def load_nodes(b, first_tile, n_tiles):
             rows = x[b].rearrange("(p j) k -> p j k", j=TILES)
@@ -127,10 +129,10 @@ def tile_hgcn_pb_t_kernel(tc, x, w_sp, out):
             nc.scalar.activation(out=squares[:], in_=us[n, i][:], func=ACT.Square, accum_out=sumsq[n][:, i : i + 1])
 
         def take_root(n):
-            clamped = small.tile([P, PAIR], F32, name="clamped")
-            nc.gpsimd.tensor_scalar(out=clamped[:], in0=sumsq[n][:], scalar1=EPS * EPS, scalar2=None, op0=ALU.max)
             radius[n] = small.tile([P, PAIR], F32, name="radius")
-            nc.gpsimd.tensor_tensor(out=radius[n][:], in0=clamped[:], in1=half[:], op=ALU.pow)
+            nc.gpsimd.tensor_tensor(out=radius[n][:], in0=sumsq[n][:], in1=half[:], op=ALU.pow)
+            clamped[n] = small.tile([P, PAIR], F32, name="clamped")
+            nc.gpsimd.tensor_scalar(out=clamped[n][:], in0=radius[n][:], scalar1=EPS, scalar2=None, op0=ALU.max)
 
         def exponentials(n):
             e_pos[n] = small.tile([P, PAIR], F32, name="e_pos")
@@ -138,19 +140,25 @@ def tile_hgcn_pb_t_kernel(tc, x, w_sp, out):
             nc.scalar.activation(out=e_pos[n][:], in_=radius[n][:], func=ACT.Exp)
             nc.scalar.activation(out=e_neg[n][:], in_=radius[n][:], func=ACT.Exp, scale=-1.0)
 
-        def factors(n):
+        def invert(n):
+            inverse[n] = small.tile([P, PAIR], F32, name="inverse")
+            nc.vector.reciprocal(out=inverse[n][:], in_=clamped[n][:])
+
+        def subtract(n):
+            diff[n] = small.tile([P, PAIR], F32, name="diff")
+            nc.vector.tensor_sub(out=diff[n][:], in0=e_pos[n][:], in1=e_neg[n][:])
+
+        def sinh_and_cosh(n):
             b, q = divmod(n, PAIRS)
             if q == 0:
                 out_sb[b] = out_pool.tile([P, TILES, 1 + DIMS], F32, name="out_sb")
-            inverse = small.tile([P, PAIR], F32, name="inverse")
-            nc.vector.reciprocal(out=inverse[:], in_=radius[n][:])
-            diff = small.tile([P, PAIR], F32, name="diff")
-            nc.vector.tensor_sub(out=diff[:], in0=e_pos[n][:], in1=e_neg[n][:])
-            factor[n] = small.tile([P, PAIR], F32, name="factor")
-            nc.vector.tensor_mul(out=factor[n][:], in0=diff[:], in1=inverse[:])
+            sinh[n] = small.tile([P, PAIR], F32, name="sinh")
+            nc.vector.tensor_scalar(
+                out=sinh[n][:], in0=diff[n][:], scalar1=TWO_SINH_EPS, scalar2=0.5, op0=ALU.max, op1=ALU.mult
+            )
             nc.vector.scalar_tensor_tensor(
                 out=out_sb[b][:, PAIR * q : PAIR * (q + 1), 0],
-                in0=diff[:],
+                in0=diff[n][:],
                 scalar=0.5,
                 in1=e_neg[n][:],
                 op0=ALU.mult,
@@ -163,35 +171,47 @@ def tile_hgcn_pb_t_kernel(tc, x, w_sp, out):
                 nc.vector.tensor_scalar(
                     out=out_sb[b][:, PAIR * q + i, 1:],
                     in0=us[n, i][:],
-                    scalar1=factor[n][:, i : i + 1],
-                    scalar2=0.5,
+                    scalar1=sinh[n][:, i : i + 1],
+                    scalar2=inverse[n][:, i : i + 1],
                     op0=ALU.mult,
                     op1=ALU.mult,
                 )
 
-        def store_graph(b):
-            nc.scalar.dma_start(out=out[b].rearrange("(p j) d -> p j d", j=TILES), in_=out_sb[b][:])
+        def store_after_pair(n):
+            b, q = divmod(n, PAIRS)
+            last_pair = q == PAIRS - 1
+            if b < GRAPHS - 1 and not last_pair:
+                return
+            first = PIECE * q if b == GRAPHS - 1 else 0
+            end = TILES * (1 + DIMS) if last_pair else PIECE * (q + 1)
+            nc.scalar.dma_start(
+                out=out[b].rearrange("(p j) d -> p (j d)", j=TILES)[:, first:end],
+                in_=out_sb[b][:].rearrange("p j d -> p (j d)")[:, first:end],
+            )
 
         def live(n):
             return 0 <= n < N_PAIRS
 
-        for s in range(N_PAIRS + 4):
-            if live(s - 4):
-                scale_pair(s - 4)
+        for s in range(N_PAIRS + 5):
             if live(s):
                 transpose_pair(s)
                 copy_out_pair(s)
-            if live(s - 1):
-                quantise_pair(s - 1)
             if live(s - 2):
                 multiply_pair(s - 2)
+            if live(s - 4):
+                scale_pair(s - 4)
+            if live(s - 2):
                 sum_squares(s - 2, 0)
+            if live(s - 5):
+                store_after_pair(s - 5)
             if live(s - 3):
+                invert(s - 3)
                 exponentials(s - 3)
+                subtract(s - 3)
             if live(s - 2):
                 sum_squares(s - 2, 1)
                 take_root(s - 2)
+            if live(s):
+                quantise_pair(s)
             if live(s - 3):
-                factors(s - 3)
-            if live(s - 4) and (s - 4) % PAIRS == PAIRS - 1:
-                store_graph((s - 4) // PAIRS)
+                sinh_and_cosh(s - 3)

@@ -21,6 +21,7 @@ PAIRS = TILES // PAIR
 N_PAIRS = GRAPHS * PAIRS
 TILE_COLS = PASSES * P * PACK
 TILE_WORDS = PASSES * P
+RUN = 4
 EPS = 1e-6
 TWO_SINH_EPS = 2.0 * EPS * (1.0 + EPS * EPS / 6.0)
 PIECE = 1024
@@ -54,10 +55,9 @@ def tile_hgcn_pb_t_kernel(tc, x, w_sp, out):
 
         load_nodes(0, 0, PAIR)
         w_raw = const.tile([P, PASSES, PACK, DIMS], BF16)
-        nc.sync.dma_start(
-            out=w_raw[:].rearrange("p g (u e) d -> p (g u) (e d)", u=HALVES),
-            in_=w_sp.rearrange("(c p e) d -> p c (e d)", c=PASSES * HALVES, p=P),
-        )
+        w_rows = w_sp.rearrange("(g u p e) d -> g p u (e d)", g=PASSES, u=HALVES, p=P)
+        for g in range(PASSES):
+            nc.sync.dma_start(out=w_raw[:, g].rearrange("p (u e) d -> p u (e d)", u=HALVES), in_=w_rows[g])
         for q in range(1, PAIRS):
             load_nodes(0, PAIR * q, PAIR)
         for b in range(1, GRAPHS):
@@ -70,7 +70,10 @@ def tile_hgcn_pb_t_kernel(tc, x, w_sp, out):
 
         w_grouped = const.tile([P, PASSES, DIMS, PACK], BF16, align_bytes=64)
         for g in range(PASSES):
-            nc.vector.tensor_copy(out=w_grouped[:, g], in_=w_raw[:, g].rearrange("p t d -> p d t"))
+            nc.vector.tensor_copy(
+                out=w_grouped[:, g].rearrange("p (c i) t -> p c t i", i=RUN),
+                in_=w_raw[:, g].rearrange("p t (c i) -> p c t i", i=RUN),
+            )
         w_codes = const.tile([P, PASSES * DIMS], U32, align_bytes=64)
         w_scales = const.tile([P, PASSES * DIMS], U8, align_bytes=64)
         nc.vector.quantize_mx(
@@ -96,7 +99,7 @@ def tile_hgcn_pb_t_kernel(tc, x, w_sp, out):
                 dst = grouped[n][:, i * TILE_COLS : (i + 1) * TILE_COLS].bitcast(F32)
                 dst = dst.rearrange("p (g r u) -> p g r u", g=PASSES, u=HALVES)
                 src = x_t[n, i][:].rearrange("p g u r -> p g r u")
-                if i == 1 and n % 2 == 1:
+                if i == 1 and n % 3 == 2:
                     nc.vector.tensor_copy(out=dst, in_=src)
                 else:
                     nc.scalar.copy(out=dst, in_=src)

@@ -21,10 +21,18 @@ PAIRS = TILES // PAIR
 N_PAIRS = GRAPHS * PAIRS
 TILE_COLS = PASSES * P * PACK
 TILE_WORDS = PASSES * P
+OUT_COLS = 1 + DIMS
 RUN = 4
 EPS = 1e-6
 TWO_SINH_EPS = 2.0 * EPS * (1.0 + EPS * EPS / 6.0)
 PIECE = 1024
+PAIRS_IN_PSUM = 3
+VECTOR_COPIES_EVERY = 3
+
+MULTIPLY_AT = 2
+EXP_AT = 3
+SCALE_AT = 4
+STORE_AT = 5
 
 FLOPS = 2 * GRAPHS * NODES * FEATURES * DIMS
 
@@ -35,10 +43,10 @@ def tile_hgcn_pb_t_kernel(tc, x, w_sp, out):
         tc.tile_pool(name="const", bufs=1) as const,
         tc.tile_pool(name="x_pool", bufs=GRAPHS) as x_pool,
         tc.tile_pool(name="out_pool", bufs=3) as out_pool,
-        tc.tile_pool(name="mx_pool", bufs=4) as mx_pool,
+        tc.tile_pool(name="mx_pool", bufs=MULTIPLY_AT + 2) as mx_pool,
         tc.tile_pool(name="small", bufs=4) as small,
         tc.psum_pool(name="xt_pool", bufs=PAIR) as xt_pool,
-        tc.psum_pool(name="us_pool", bufs=3 * PAIR) as us_pool,
+        tc.psum_pool(name="us_pool", bufs=PAIRS_IN_PSUM * PAIR) as us_pool,
         tc.manual_schedule(),
     ):
         x_sb, out_sb = {}, {}
@@ -53,11 +61,12 @@ def tile_hgcn_pb_t_kernel(tc, x, w_sp, out):
         for b in range(GRAPHS):
             x_sb[b] = x_pool.tile([P, TILES, FEATURES], BF16, name="x_sb")
 
-        load_nodes(0, 0, PAIR)
+        load_nodes(0, 0, 1)
         w_raw = const.tile([P, PASSES, PACK, DIMS], BF16)
         w_rows = w_sp.rearrange("(g u p e) d -> g p u (e d)", g=PASSES, u=HALVES, p=P)
         for g in range(PASSES):
             nc.sync.dma_start(out=w_raw[:, g].rearrange("p (u e) d -> p u (e d)", u=HALVES), in_=w_rows[g])
+        load_nodes(0, 1, 1)
         for q in range(1, PAIRS):
             load_nodes(0, PAIR * q, PAIR)
         for b in range(1, GRAPHS):
@@ -99,7 +108,7 @@ def tile_hgcn_pb_t_kernel(tc, x, w_sp, out):
                 dst = grouped[n][:, i * TILE_COLS : (i + 1) * TILE_COLS].bitcast(F32)
                 dst = dst.rearrange("p (g r u) -> p g r u", g=PASSES, u=HALVES)
                 src = x_t[n, i][:].rearrange("p g u r -> p g r u")
-                if i == 1 and n % 3 == 2:
+                if i == PAIR - 1 and n % VECTOR_COPIES_EVERY == VECTOR_COPIES_EVERY - 1:
                     nc.vector.tensor_copy(out=dst, in_=src)
                 else:
                     nc.scalar.copy(out=dst, in_=src)
@@ -154,7 +163,7 @@ def tile_hgcn_pb_t_kernel(tc, x, w_sp, out):
         def sinh_and_cosh(n):
             b, q = divmod(n, PAIRS)
             if q == 0:
-                out_sb[b] = out_pool.tile([P, TILES, 1 + DIMS], F32, name="out_sb")
+                out_sb[b] = out_pool.tile([P, TILES, OUT_COLS], F32, name="out_sb")
             sinh[n] = small.tile([P, PAIR], F32, name="sinh")
             nc.vector.tensor_scalar(
                 out=sinh[n][:], in0=diff[n][:], scalar1=TWO_SINH_EPS, scalar2=0.5, op0=ALU.max, op1=ALU.mult
@@ -174,8 +183,8 @@ def tile_hgcn_pb_t_kernel(tc, x, w_sp, out):
                 nc.vector.tensor_scalar(
                     out=out_sb[b][:, PAIR * q + i, 1:],
                     in0=us[n, i][:],
-                    scalar1=sinh[n][:, i : i + 1],
-                    scalar2=inverse[n][:, i : i + 1],
+                    scalar1=inverse[n][:, i : i + 1],
+                    scalar2=sinh[n][:, i : i + 1],
                     op0=ALU.mult,
                     op1=ALU.mult,
                 )
@@ -186,7 +195,7 @@ def tile_hgcn_pb_t_kernel(tc, x, w_sp, out):
             if b < GRAPHS - 1 and not last_pair:
                 return
             first = PIECE * q if b == GRAPHS - 1 else 0
-            end = TILES * (1 + DIMS) if last_pair else PIECE * (q + 1)
+            end = TILES * OUT_COLS if last_pair else PIECE * (q + 1)
             nc.scalar.dma_start(
                 out=out[b].rearrange("(p j) d -> p (j d)", j=TILES)[:, first:end],
                 in_=out_sb[b][:].rearrange("p j d -> p (j d)")[:, first:end],
@@ -195,26 +204,26 @@ def tile_hgcn_pb_t_kernel(tc, x, w_sp, out):
         def live(n):
             return 0 <= n < N_PAIRS
 
-        for s in range(N_PAIRS + 5):
+        for s in range(N_PAIRS + STORE_AT):
             if live(s):
                 transpose_pair(s)
                 copy_out_pair(s)
-            if live(s - 2):
-                multiply_pair(s - 2)
-            if live(s - 4):
-                scale_pair(s - 4)
-            if live(s - 2):
-                sum_squares(s - 2, 0)
-            if live(s - 5):
-                store_after_pair(s - 5)
-            if live(s - 3):
-                invert(s - 3)
-                exponentials(s - 3)
-                subtract(s - 3)
-            if live(s - 2):
-                sum_squares(s - 2, 1)
-                take_root(s - 2)
+            if live(s - MULTIPLY_AT):
+                multiply_pair(s - MULTIPLY_AT)
+            if live(s - SCALE_AT):
+                scale_pair(s - SCALE_AT)
+            if live(s - MULTIPLY_AT):
+                sum_squares(s - MULTIPLY_AT, 0)
+            if live(s - STORE_AT):
+                store_after_pair(s - STORE_AT)
+            if live(s - EXP_AT):
+                invert(s - EXP_AT)
+                exponentials(s - EXP_AT)
+                subtract(s - EXP_AT)
+            if live(s - MULTIPLY_AT):
+                sum_squares(s - MULTIPLY_AT, 1)
+                take_root(s - MULTIPLY_AT)
             if live(s):
                 quantise_pair(s)
-            if live(s - 3):
-                sinh_and_cosh(s - 3)
+            if live(s - EXP_AT):
+                sinh_and_cosh(s - EXP_AT)

import concourse.mybir as mybir
from concourse.masks import make_identity

BF16 = mybir.dt.bfloat16
F32 = mybir.dt.float32
U32 = mybir.dt.uint32
U8 = mybir.dt.uint8
FP8X4 = mybir.dt.float8_e4m3fn_x4
ACT = mybir.ActivationFunctionType
ALU = mybir.AluOpType

P = 128
GRAPHS, NODES, FEATURES, DIMS = 8, 1024, 1024, 512
PACK = 4
K_PASS = P * PACK
PASSES = FEATURES // K_PASS
HALVES = 2
TILES = NODES // P
PAIR = 2
PAIRS = TILES // PAIR
N_PAIRS = GRAPHS * PAIRS
TILE_COLS = PASSES * P * PACK
TILE_WORDS = PASSES * P
OUT_COLS = 1 + DIMS
RUN = 4
EPS = 1e-6
TWO_SINH_EPS = 2.0 * EPS * (1.0 + EPS * EPS / 6.0)
PIECE = 1024
PAIRS_IN_PSUM = 3
VECTOR_COPIES_EVERY = 3

MULTIPLY_AT = 2
EXP_AT = 3
SCALE_AT = 4
STORE_AT = 5

FLOPS = 2 * GRAPHS * NODES * FEATURES * DIMS


def tile_hgcn_pb_t_kernel(tc, x, w_sp, out):
    nc = tc.nc
    with (
        tc.tile_pool(name="const", bufs=1) as const,
        tc.tile_pool(name="x_pool", bufs=GRAPHS) as x_pool,
        tc.tile_pool(name="out_pool", bufs=3) as out_pool,
        tc.tile_pool(name="mx_pool", bufs=MULTIPLY_AT + 2) as mx_pool,
        tc.tile_pool(name="small", bufs=4) as small,
        tc.psum_pool(name="xt_pool", bufs=PAIR) as xt_pool,
        tc.psum_pool(name="us_pool", bufs=PAIRS_IN_PSUM * PAIR) as us_pool,
        tc.manual_schedule(),
    ):
        x_sb, out_sb = {}, {}
        x_t, grouped, codes, scales, us = {}, {}, {}, {}, {}
        sumsq, radius, clamped, e_pos, e_neg, inverse, diff, sinh = {}, {}, {}, {}, {}, {}, {}, {}

        def load_nodes(b, first_tile, n_tiles):
            rows = x[b].rearrange("(p j) k -> p j k", j=TILES)
            cut = slice(first_tile, first_tile + n_tiles)
            nc.sync.dma_start(out=x_sb[b][:, cut, :], in_=rows[:, cut, :])

        for b in range(GRAPHS):
            x_sb[b] = x_pool.tile([P, TILES, FEATURES], BF16, name="x_sb")

        load_nodes(0, 0, 1)
        w_raw = const.tile([P, PASSES, PACK, DIMS], BF16)
        w_rows = w_sp.rearrange("(g u p e) d -> g p u (e d)", g=PASSES, u=HALVES, p=P)
        for g in range(PASSES):
            nc.sync.dma_start(out=w_raw[:, g].rearrange("p (u e) d -> p u (e d)", u=HALVES), in_=w_rows[g])
        load_nodes(0, 1, 1)
        for q in range(1, PAIRS):
            load_nodes(0, PAIR * q, PAIR)
        for b in range(1, GRAPHS):
            load_nodes(b, 0, TILES)

        ident = const.tile([P, P], F32)
        make_identity(nc, ident[:])
        half = const.tile([P, PAIR], F32)
        nc.gpsimd.memset(half[:], 0.5)

        w_grouped = const.tile([P, PASSES, DIMS, PACK], BF16, align_bytes=64)
        for g in range(PASSES):
            nc.vector.tensor_copy(
                out=w_grouped[:, g].rearrange("p (c i) t -> p c t i", i=RUN),
                in_=w_raw[:, g].rearrange("p t (c i) -> p c t i", i=RUN),
            )
        w_codes = const.tile([P, PASSES * DIMS], U32, align_bytes=64)
        w_scales = const.tile([P, PASSES * DIMS], U8, align_bytes=64)
        nc.vector.quantize_mx(
            out=w_codes[:].bitcast(FP8X4),
            scales=w_scales[:],
            in_=w_grouped[:].rearrange("p g d t -> p (g d t)"),
        )

        def transpose_pair(n):
            b, q = divmod(n, PAIRS)
            for i in range(PAIR):
                words = x_sb[b][:, PAIR * q + i, :].bitcast(F32)
                bank = xt_pool.tile([P, PASSES, HALVES, P], F32, name="x_t")
                for g in range(PASSES):
                    for u in range(HALVES):
                        first = (g * HALVES + u) * P
                        nc.tensor.transpose(bank[:, g, u, :], words[:, first : first + P], ident[:])
                x_t[n, i] = bank

        def copy_out_pair(n):
            grouped[n] = mx_pool.tile([P, PAIR * TILE_COLS], BF16, align_bytes=64, name="grouped")
            for i in range(PAIR):
                dst = grouped[n][:, i * TILE_COLS : (i + 1) * TILE_COLS].bitcast(F32)
                dst = dst.rearrange("p (g r u) -> p g r u", g=PASSES, u=HALVES)
                src = x_t[n, i][:].rearrange("p g u r -> p g r u")
                if i == PAIR - 1 and n % VECTOR_COPIES_EVERY == VECTOR_COPIES_EVERY - 1:
                    nc.vector.tensor_copy(out=dst, in_=src)
                else:
                    nc.scalar.copy(out=dst, in_=src)

        def quantise_pair(n):
            codes[n] = mx_pool.tile([P, PAIR * TILE_WORDS], U32, align_bytes=64, name="codes")
            scales[n] = mx_pool.tile([P, PAIR * TILE_WORDS], U8, align_bytes=64, name="scales")
            nc.vector.quantize_mx(out=codes[n][:].bitcast(FP8X4), scales=scales[n][:], in_=grouped[n][:])

        def multiply_pair(n):
            for i in range(PAIR):
                us[n, i] = us_pool.tile([P, DIMS], F32, name="us")
                for g in range(PASSES):
                    nodes = slice((i * PASSES + g) * P, (i * PASSES + g + 1) * P)
                    dims = slice(g * DIMS, (g + 1) * DIMS)
                    nc.tensor.matmul_mx(
                        out=us[n, i][:],
                        lhsT=codes[n][:, nodes].bitcast(FP8X4),
                        lhsT_scale=scales[n][:, nodes],
                        rhs=w_codes[:, dims].bitcast(FP8X4),
                        rhs_scale=w_scales[:, dims],
                        start=(g == 0),
                        stop=(g == PASSES - 1),
                    )

        def sum_squares(n, i):
            if i == 0:
                sumsq[n] = small.tile([P, PAIR], F32, name="sumsq")
            squares = small.tile([P, DIMS], BF16, name="squares")
            nc.scalar.activation(out=squares[:], in_=us[n, i][:], func=ACT.Square, accum_out=sumsq[n][:, i : i + 1])

        def take_root(n):
            radius[n] = small.tile([P, PAIR], F32, name="radius")
            nc.gpsimd.tensor_tensor(out=radius[n][:], in0=sumsq[n][:], in1=half[:], op=ALU.pow)
            clamped[n] = small.tile([P, PAIR], F32, name="clamped")
            nc.gpsimd.tensor_scalar(out=clamped[n][:], in0=radius[n][:], scalar1=EPS, scalar2=None, op0=ALU.max)

        def exponentials(n):
            e_pos[n] = small.tile([P, PAIR], F32, name="e_pos")
            e_neg[n] = small.tile([P, PAIR], F32, name="e_neg")
            nc.scalar.activation(out=e_pos[n][:], in_=radius[n][:], func=ACT.Exp)
            nc.scalar.activation(out=e_neg[n][:], in_=radius[n][:], func=ACT.Exp, scale=-1.0)

        def invert(n):
            inverse[n] = small.tile([P, PAIR], F32, name="inverse")
            nc.vector.reciprocal(out=inverse[n][:], in_=clamped[n][:])

        def subtract(n):
            diff[n] = small.tile([P, PAIR], F32, name="diff")
            nc.vector.tensor_sub(out=diff[n][:], in0=e_pos[n][:], in1=e_neg[n][:])

        def sinh_and_cosh(n):
            b, q = divmod(n, PAIRS)
            if q == 0:
                out_sb[b] = out_pool.tile([P, TILES, OUT_COLS], F32, name="out_sb")
            sinh[n] = small.tile([P, PAIR], F32, name="sinh")
            nc.vector.tensor_scalar(
                out=sinh[n][:], in0=diff[n][:], scalar1=TWO_SINH_EPS, scalar2=0.5, op0=ALU.max, op1=ALU.mult
            )
            nc.vector.scalar_tensor_tensor(
                out=out_sb[b][:, PAIR * q : PAIR * (q + 1), 0],
                in0=diff[n][:],
                scalar=0.5,
                in1=e_neg[n][:],
                op0=ALU.mult,
                op1=ALU.add,
            )

        def scale_pair(n):
            b, q = divmod(n, PAIRS)
            for i in range(PAIR):
                nc.vector.tensor_scalar(
                    out=out_sb[b][:, PAIR * q + i, 1:],
                    in0=us[n, i][:],
                    scalar1=inverse[n][:, i : i + 1],
                    scalar2=sinh[n][:, i : i + 1],
                    op0=ALU.mult,
                    op1=ALU.mult,
                )

        def store_after_pair(n):
            b, q = divmod(n, PAIRS)
            last_pair = q == PAIRS - 1
            if b < GRAPHS - 1 and not last_pair:
                return
            first = PIECE * q if b == GRAPHS - 1 else 0
            end = TILES * OUT_COLS if last_pair else PIECE * (q + 1)
            nc.scalar.dma_start(
                out=out[b].rearrange("(p j) d -> p (j d)", j=TILES)[:, first:end],
                in_=out_sb[b][:].rearrange("p j d -> p (j d)")[:, first:end],
            )

        def live(n):
            return 0 <= n < N_PAIRS

        for s in range(N_PAIRS + STORE_AT):
            if live(s):
                transpose_pair(s)
                copy_out_pair(s)
            if live(s - MULTIPLY_AT):
                multiply_pair(s - MULTIPLY_AT)
            if live(s - SCALE_AT):
                scale_pair(s - SCALE_AT)
            if live(s - MULTIPLY_AT):
                sum_squares(s - MULTIPLY_AT, 0)
            if live(s - STORE_AT):
                store_after_pair(s - STORE_AT)
            if live(s - EXP_AT):
                invert(s - EXP_AT)
                exponentials(s - EXP_AT)
                subtract(s - EXP_AT)
            if live(s - MULTIPLY_AT):
                sum_squares(s - MULTIPLY_AT, 1)
                take_root(s - MULTIPLY_AT)
            if live(s):
                quantise_pair(s)
            if live(s - EXP_AT):
                sinh_and_cosh(s - EXP_AT)
